import numpy as np
import ml_dtypes


def mxq(x, axis, fmt="e4m3"):
    dtype, down = {"e4m3": (ml_dtypes.float8_e4m3fn, 7), "e5m2": (ml_dtypes.float8_e5m2, 14)}[fmt]
    v = np.moveaxis(np.asarray(x, np.float32).astype(ml_dtypes.bfloat16).astype(np.float64), axis, -1)
    blocks = v.reshape(v.shape[:-1] + (-1, 32))
    amax = np.abs(blocks).max(-1, keepdims=True)
    byte = np.maximum(np.where(amax > 0, np.frexp(amax)[1] - 1 + 127, 0) - down, 1)
    scale = np.exp2(byte - 127.0)
    codes = (blocks / scale).astype(np.float32).astype(dtype).astype(np.float64)
    return np.moveaxis((codes * scale).reshape(v.shape), -1, axis)


WIDE = False


def mx_kscale(k):
    if not WIDE:
        return np.ones(k)
    levels = np.array([10, -10, 5, -5, 0])
    if k % 512:
        return np.exp2(np.random.permutation(np.resize(levels, k // 32))).repeat(32)
    a = np.empty((k // 512, 16))
    for p in range(k // 512):
        a[p, :8] = np.random.permutation(np.resize(levels, 8))
        for g in range(8):
            far = levels[np.abs(levels - a[p, g]) >= 10]
            a[p, g + 8] = far[np.random.randint(len(far))]
    return np.exp2(a.ravel()).repeat(32)


BF16 = ml_dtypes.bfloat16


def bf(x):
    return np.asarray(x, np.float32).astype(BF16)


def f64(x):
    return np.asarray(x).astype(np.float64)


B, S, D, R = 2, 1024, 1024, 8
EPS = 1e-6


def draw0():
    s, t = mx_kscale(D), mx_kscale(D)
    return {"x": bf(np.random.standard_normal((B, S, D)) * s),
            "pos_emb": bf(np.random.standard_normal((1, S, D)) * s),
            "enc_w0": bf(np.random.standard_normal((D, D)) / np.sqrt(D) / s[None, :] * t[:, None]),
            "enc_w1": bf(np.random.standard_normal((D, D)) / np.sqrt(D) / t[None, :])}


def core(x, pos_emb, enc_w0, enc_w1):
    x = f64(x)
    y = x + f64(pos_emb)[:, : x.shape[1]]
    h = np.maximum(mxq(y, 2, "e4m3") @ mxq(f64(enc_w0), 1, "e4m3").T, 0.0)
    h = np.maximum(mxq(h, 2, "e4m3") @ mxq(f64(enc_w1), 1, "e4m3").T, 0.0)
    return h / (np.sqrt((h * h).sum(-1, keepdims=True)) + EPS)


def e4m3fn_bytes(y):
    return np.clip(np.asarray(y, np.float64), -448.0, 448.0).astype(np.float32).astype(ml_dtypes.float8_e4m3fn).view(np.uint8)


def e4m3fn_values(b):
    return np.asarray(b, np.uint8).view(ml_dtypes.float8_e4m3fn).astype(np.float64)


def setup_inputs():
    d = draw0()
    x0 = np.asarray(d['enc_w1']).astype(np.float64)
    s = (np.max(np.abs(x0), axis=(0,), keepdims=True) / 448.0).astype(np.float32)
    out = {}
    for k, v in d.items():
        if k == 'enc_w1':
            out['enc_w1_bytes'] = e4m3fn_bytes(x0 / s.astype(np.float64))
            out['enc_w1_scale'] = s
        else:
            out[k] = v
    return out


def reference(x, pos_emb, enc_w0, enc_w1_bytes, enc_w1_scale):
    return core(x, pos_emb, enc_w0, e4m3fn_values(enc_w1_bytes) * enc_w1_scale.astype(np.float64))

from contextlib import ExitStack

import concourse.mybir as mybir
from concourse.masks import make_identity

B, S, D = 2, 1024, 1024
EPS = 1e-6
FLOPS = 2 * (2 * B * S * D * D)

F32 = mybir.dt.float32
BF16 = mybir.dt.bfloat16
U32 = mybir.dt.uint32
U8 = mybir.dt.uint8
FP8 = mybir.dt.float8_e4m3fn
FP8X4 = mybir.dt.float8_e4m3fn_x4
ADD = mybir.AluOpType.add
MULT = mybir.AluOpType.mult
MAX = mybir.AluOpType.max
ACT = mybir.ActivationFunctionType

P = 128
PASSES = 2
TILES = B * S // P
HEAD = 9


def tile_mybadtransfomerblock_pa_kernel(tc, x, pos_emb, enc_w0, enc_w1_bytes, enc_w1_scale, out):
    nc = tc.nc
    with ExitStack() as ctx:
        keep = ctx.enter_context(tc.tile_pool(name="keep", bufs=1))
        work = ctx.enter_context(tc.tile_pool(name="work", bufs=3))
        psum = ctx.enter_context(tc.psum_pool(name="psum", bufs=8))

        ident = keep.tile([P, P], F32, tag="ident")
        make_identity(nc, ident[:])
        warm = keep.tile([P, 1], F32, tag="warm")
        nc.vector.memset(warm[:], 1.0)
        warm2 = keep.tile([P, 1], F32, tag="warm2")
        nc.scalar.activation(out=warm2[:], in_=warm[:], func=ACT.Sqrt)

        x_in, pos_in, w0_in, yp, yt, y_codes, y_scales = {}, {}, {}, {}, {}, {}, {}
        ht, h_codes, h_scales, bank, res, sums, inv = {}, {}, {}, {}, {}, {}, {}
        w1_prod = {}

        w1_in = keep.tile([P, 8, D], U8, tag="w1_in")
        w1_scale = keep.tile([P, D], F32, tag="w1_scale")
        w0_codes = keep.tile([P, 8, PASSES, P], U32, tag="w0_codes", align_bytes=64)
        w0_scales = keep.tile([P, 8, PASSES, P], U8, tag="w0_scales", align_bytes=64)
        w1_grouped = keep.tile([P, PASSES, D, 4], BF16, tag="w1_grouped", align_bytes=64)
        w1_codes = keep.tile([P, PASSES, D], U32, tag="w1_codes", align_bytes=64)
        w1_scales = keep.tile([P, PASSES, D], U8, tag="w1_scales", align_bytes=64)

        def load_x(i):
            x_in[i] = work.tile([P, D], BF16, tag="x_in", bufs=TILES, name="x_in")
            s0 = (i // 2) * P
            nc.sync.dma_start(out=x_in[i][:], in_=x[i % 2, s0 : s0 + P, :])

        def load_pos(j):
            pos_in[j] = work.tile([P, D], BF16, tag="pos_in", bufs=8, name="pos_in")
            nc.sync.dma_start(out=pos_in[j][:], in_=pos_emb[0, j * P : (j + 1) * P, :])

        w0_rows = enc_w0.rearrange("(h m t) k -> h t m k", h=2, m=P, t=4)

        def load_w0(c):
            w0_in[c] = work.tile([P, D], BF16, tag="w0_in", bufs=8, name="w0_in")
            nc.sync.dma_start(out=w0_in[c][:], in_=w0_rows[c // 4, c % 4])

        w1_rows = enc_w1_bytes.rearrange("(a m) k -> m a k", m=P)

        def load_w1(a, n):
            nc.sync.dma_start(out=w1_in[:, a : a + n, :], in_=w1_rows[:, a : a + n, :])

        def new_bank(key):
            bank[key] = psum.tile([P, 512], F32, tag="bank", name="bank")
            return bank[key]

        def transpose_words(key, words, stepped):
            b = new_bank(key)
            v = b[:].rearrange("p (g u n) -> p g u n", g=2, u=2)
            for g in range(2):
                for u in range(2):
                    if stepped:
                        src = words[:, 256 * g + u : 256 * (g + 1) : 2]
                    else:
                        src = words[:, 256 * u + 128 * g : 256 * u + 128 * (g + 1)]
                    nc.tensor.transpose(v[:, g, u, :], src, ident[:])

        def copy_words(engine, key, dst):
            src = bank.pop(key)[:].rearrange("p (g u n) -> p g n u", g=2, u=2)
            if engine == "s":
                nc.scalar.copy(out=dst, in_=src)
            else:
                nc.vector.tensor_copy(out=dst, in_=src)

        def add_pos(i):
            yp[i] = work.tile([P, D], BF16, tag="yp", name="yp")
            pairs = "p (w u e) -> p w u e"
            nc.vector.tensor_tensor(
                out=yp[i][:].rearrange("p (u w e) -> p w u e", u=2, e=2),
                in0=x_in.pop(i)[:].rearrange(pairs, u=2, e=2),
                in1=pos_in[i // 2][:].rearrange(pairs, u=2, e=2),
                op=ADD,
            )

        def transpose_y(i):
            transpose_words(("y", i), yp.pop(i)[:].bitcast(F32), False)

        def copy_y(i, engine):
            yt[i] = work.tile([P, D], BF16, tag="yt", name="yt", align_bytes=64)
            copy_words(engine, ("y", i), yt[i][:].bitcast(F32).rearrange("p (g n u) -> p g n u", g=2, u=2))

        def quant_y(i):
            y_codes[i] = work.tile([P, 256], U32, tag="y_codes", name="y_codes", align_bytes=64, bufs=4)
            y_scales[i] = work.tile([P, 256], U8, tag="y_scales", name="y_scales", align_bytes=64, bufs=4)
            nc.vector.quantize_mx(out=y_codes[i][:].bitcast(FP8X4), scales=y_scales[i][:], in_=yt.pop(i)[:])

        w0_grouped = {}

        def transpose_w0(c):
            transpose_words(("w0", c), w0_in.pop(c)[:].bitcast(F32), True)

        def copy_w0(c, engine):
            w0_grouped[c] = work.tile([P, D], BF16, tag="w0_grouped", name="w0_grouped", align_bytes=64)
            copy_words(engine, ("w0", c), w0_grouped[c][:].bitcast(F32).rearrange("p (g n u) -> p g n u", g=2, u=2))

        def quant_w0(c):
            nc.vector.quantize_mx(
                out=w0_codes[:, c].rearrange("p g m -> p (g m)").bitcast(FP8X4),
                scales=w0_scales[:, c].rearrange("p g m -> p (g m)"),
                in_=w0_grouped.pop(c)[:],
            )

        def scale_w1(a):
            w1_prod[a] = work.tile([P, D], BF16, tag="w1_prod", name="w1_prod")
            nc.vector.tensor_tensor(out=w1_prod[a][:], in0=w1_in[:, a, :].bitcast(FP8), in1=w1_scale[:], op=MULT)

        def transpose_w1(a):
            transpose_words(("w1", a), w1_prod.pop(a)[:].bitcast(F32), True)

        def copy_w1(a, engine):
            dst = w1_grouped[:, :, a * P : (a + 1) * P, :].rearrange("p g n t -> p g (n t)").bitcast(F32)
            copy_words(engine, ("w1", a), dst.rearrange("p g (n u) -> p g n u", u=2))

        def quant_w1(pair):
            cols = slice(pair * 256, (pair + 1) * 256)
            for g in range(2):
                nc.vector.quantize_mx(
                    out=w1_codes[:, g, cols].bitcast(FP8X4),
                    scales=w1_scales[:, g, cols],
                    in_=w1_grouped[:, g, cols, :].rearrange("p n t -> p (n t)"),
                )

        def stage1(i, h):
            yc, ys = y_codes[i], y_scales[i]
            b = new_bank(("h", i, h))
            for t in range(4):
                for g in range(2):
                    nc.tensor.matmul_mx(
                        out=b[:, t * P : (t + 1) * P],
                        lhsT=w0_codes[:, 4 * h + t, g, :].bitcast(FP8X4),
                        lhsT_scale=w0_scales[:, 4 * h + t, g, :],
                        rhs=yc[:, g * P : (g + 1) * P].bitcast(FP8X4),
                        rhs_scale=ys[:, g * P : (g + 1) * P],
                        start=(g == 0),
                        stop=(g == 1),
                    )

        def relu_h(i, h, engine):
            if h == 0:
                ht[i] = work.tile([P, 2, P, 4], BF16, tag="ht", name="ht", align_bytes=64)
            src = bank.pop(("h", i, h))[:].rearrange("p (t n) -> p n t", t=4)
            dst = ht[i][:, h]
            if engine == "s":
                nc.scalar.activation(out=dst, in_=src, func=ACT.Relu)
            else:
                nc.vector.tensor_scalar(out=dst, in0=src, scalar1=0.0, scalar2=None, op0=MAX)

        def quant_h(i):
            h_codes[i] = work.tile([P, 256], U32, tag="h_codes", name="h_codes", align_bytes=64, bufs=12)
            h_scales[i] = work.tile([P, 256], U8, tag="h_scales", name="h_scales", align_bytes=64, bufs=12)
            nc.vector.quantize_mx(
                out=h_codes[i][:].bitcast(FP8X4),
                scales=h_scales[i][:],
                in_=ht.pop(i)[:].rearrange("p h n t -> p (h n t)"),
            )

        def stage2(i, n):
            hc, hs = h_codes[i], h_scales[i]
            b = new_bank(("o", i, n))
            for h in range(2):
                nc.tensor.matmul_mx(
                    out=b[:],
                    lhsT=hc[:, h * P : (h + 1) * P].bitcast(FP8X4),
                    lhsT_scale=hs[:, h * P : (h + 1) * P],
                    rhs=w1_codes[:, h, n * 512 : (n + 1) * 512].bitcast(FP8X4),
                    rhs_scale=w1_scales[:, h, n * 512 : (n + 1) * 512],
                    start=(h == 0),
                    stop=(h == 1),
                )

        def relu_out(i, n, engine):
            if n == 0:
                res[i] = work.tile([P, D], F32, tag="res", name="res", bufs=8)
            src = bank.pop(("o", i, n))[:]
            dst = res[i][:, n * 512 : (n + 1) * 512]
            if engine == "s":
                nc.scalar.activation(out=dst, in_=src, func=ACT.Relu)
            else:
                nc.vector.tensor_scalar(out=dst, in0=src, scalar1=0.0, scalar2=None, op0=MAX)

        def squares(i, n, engine):
            if i not in sums:
                sums[i] = work.tile([P, 2], F32, tag="sums", name="sums", bufs=6)
            cols = slice(0, D) if n is None else slice(n * 512, (n + 1) * 512)
            acc = sums[i][:, n or 0 : (n or 0) + 1]
            part = res[i][:, cols]
            if engine == "s":
                junk_s = work.tile([P, D], F32, tag="junk_s", name="junk_s", bufs=2)
                nc.scalar.activation(out=junk_s[:, cols], in_=part, func=ACT.Square, accum_out=acc)
            else:
                junk_v = work.tile([P, D], F32, tag="junk_v", name="junk_v", bufs=2)
                nc.vector.scalar_tensor_tensor(
                    out=junk_v[:, cols], in0=part, scalar=1.0, in1=part, op0=MULT, op1=MULT, accum_out=acc
                )

        def root(i, halves):
            inv[i] = work.tile([P, 1], F32, tag="inv", name="inv", bufs=6)
            if halves:
                nc.scalar.activation(out=inv[i][:], in_=sums[i][:, 0:1], func=ACT.Sqrt, bias=sums[i][:, 1:2])
            else:
                nc.scalar.activation(out=inv[i][:], in_=sums[i][:, 0:1], func=ACT.Sqrt)

        def add_eps(i):
            nc.vector.tensor_scalar(out=inv[i][:], in0=inv[i][:], scalar1=EPS, scalar2=None, op0=ADD)

        def reciprocal(i):
            nc.vector.reciprocal(out=inv[i][:], in_=inv[i][:])

        def scale_store(i, n, engine):
            cols = slice(0, D) if n is None else slice(n * 512, (n + 1) * 512)
            r = res[i][:, cols]
            if engine == "v":
                nc.vector.tensor_scalar(out=r, in0=r, scalar1=inv[i][:], scalar2=None, op0=MULT)
            elif engine == "g":
                nc.gpsimd.tensor_scalar(out=r, in0=r, scalar1=inv[i][:], scalar2=0.0, op0=MULT, op1=ADD)
            else:
                nc.scalar.activation(out=r, in_=r, func=ACT.Copy, scale=inv[i][:])
            s0 = (i // 2) * P
            nc.sync.dma_start(out=out[i % 2, s0 : s0 + P, cols], in_=r)

        load_w0(0)
        load_x(0)
        load_pos(0)
        for c in range(1, 4):
            load_w0(c)
        load_x(1)
        for c in range(4, 8):
            load_w0(c)
        load_x(2)
        load_pos(1)
        nc.sync.dma_start(out=w1_scale[:], in_=enc_w1_scale.rearrange("o k -> (o k)").partition_broadcast(P))
        load_w1(0, 2)
        load_x(3)
        load_w1(2, 2)
        load_x(4)
        load_pos(2)
        load_w1(4, 2)
        load_x(5)
        load_w1(6, 2)
        for i in range(6, TILES):
            load_x(i)
            if i % 2 == 0:
                load_pos(i // 2)

        transpose_w0(0)
        copy_w0(0, "s")
        add_pos(0)
        quant_w0(0)
        transpose_y(0)
        transpose_w0(1)
        copy_y(0, "s")
        copy_w0(1, "s")
        transpose_w0(2)
        copy_w0(2, "s")
        quant_w0(1)
        quant_y(0)
        transpose_w0(3)
        copy_w0(3, "s")
        quant_w0(2)
        add_pos(1)
        transpose_y(1)
        quant_w0(3)
        copy_y(1, "s")
        transpose_w0(4)
        copy_w0(4, "s")
        stage1(0, 0)
        transpose_w0(5)
        copy_w0(5, "s")
        quant_y(1)
        quant_w0(4)
        transpose_w0(6)
        copy_w0(6, "s")
        quant_w0(5)
        transpose_w0(7)
        copy_w0(7, "v")
        quant_w0(6)
        add_pos(2)
        quant_w0(7)
        relu_h(0, 0, "s")
        stage1(1, 0)
        stage1(0, 1)
        transpose_y(2)
        relu_h(1, 0, "s")
        relu_h(0, 1, "s")
        stage1(1, 1)
        copy_y(2, "s")
        scale_w1(0)
        quant_h(0)
        add_pos(3)
        quant_y(2)
        relu_h(1, 1, "s")

        for s in range(1, HEAD):
            transpose_w1(s - 1)
            transpose_y(s + 2)
            copy_w1(s - 1, "s")
            if s < 8:
                scale_w1(s)
            stage1(s + 1, 0)
            stage1(s + 1, 1)
            copy_y(s + 2, "s")
            quant_h(s)
            relu_h(s + 1, 0, "s")
            add_pos(s + 3)
            relu_h(s + 1, 1, "s")
            if s % 2 == 0:
                quant_w1(s // 2 - 1)
            quant_y(s + 2)
            if s >= 6:
                stage2(s - 6, 0)
                relu_out(s - 6, 0, "s")

        transpose_y(HEAD + 2)
        quant_h(HEAD)

        started = 3
        for q in range(10):
            a, b = 2 * q, 2 * q + 1
            i = HEAD + 1 + q
            if a < TILES:
                if a >= started:
                    stage2(a, 0)
                stage2(a, 1)
            if i < TILES:
                stage1(i, 0)
                stage1(i, 1)
            if i + 1 < TILES:
                copy_y(i + 1, "v")
            if a < TILES and a >= started:
                relu_out(a, 0, "s")
            if a < TILES:
                relu_out(a, 1, "v")
            if i + 2 < TILES:
                add_pos(i + 2)
                transpose_y(i + 2)
            if i + 1 < TILES:
                quant_y(i + 1)
            if i < TILES:
                relu_h(i, 0, "s")
                relu_h(i, 1, "v")
            if b < TILES:
                if b >= started:
                    stage2(b, 0)
                stage2(b, 1)
            for j in (a - 2, a - 1):
                if 0 <= j < TILES - 2:
                    squares(j, None, "s")
                    root(j, False)
                elif TILES - 2 <= j < TILES:
                    squares(j, 0, "s")
                    squares(j, 1, "v")
                    root(j, True)
            if i < TILES:
                quant_h(i)
            if b < TILES:
                if b >= started:
                    relu_out(b, 0, "s")
                relu_out(b, 1, "s" if q % 3 == 0 and q < 6 else "v")
            for j in (a - 2, a - 1):
                if 0 <= j < TILES:
                    add_eps(j)
                    reciprocal(j)
                    if j < TILES - 2:
                        scale_store(j, None, "v")
                    else:
                        scale_store(j, 0, "v")
                        scale_store(j, 1, "s")
